import numpy as np
import ml_dtypes


def mxq(x, axis, fmt="e4m3"):
    dtype, down = {"e4m3": (ml_dtypes.float8_e4m3fn, 7), "e5m2": (ml_dtypes.float8_e5m2, 14)}[fmt]
    v = np.moveaxis(np.asarray(x, np.float32).astype(ml_dtypes.bfloat16).astype(np.float64), axis, -1)
    blocks = v.reshape(v.shape[:-1] + (-1, 32))
    amax = np.abs(blocks).max(-1, keepdims=True)
    byte = np.maximum(np.where(amax > 0, np.frexp(amax)[1] - 1 + 127, 0) - down, 1)
    scale = np.exp2(byte - 127.0)
    codes = (blocks / scale).astype(np.float32).astype(dtype).astype(np.float64)
    return np.moveaxis((codes * scale).reshape(v.shape), -1, axis)


WIDE = False


def mx_kscale(k):
    if not WIDE:
        return np.ones(k)
    levels = np.array([10, -10, 5, -5, 0])
    a = np.random.permutation(np.resize(levels, k // 512 * 4)).reshape(k // 512, 4)
    idx = np.arange(k)
    return np.exp2(a[idx // 512, idx % 128 // 32])


BF16 = ml_dtypes.bfloat16


def bf(x):
    return np.asarray(x, np.float32).astype(BF16)


def f64(x):
    return np.asarray(x).astype(np.float64)


B, H, W, L, R, F = 2, 8, 8, 2, 512, 512
E = L * R
P = B * H * W
WIN = 2


def new_gelu(v):
    return 0.5 * v * (1.0 + np.tanh(np.sqrt(2.0 / np.pi) * (v + 0.044715 * v * v * v)))


def avg_siblings(v, order):
    side = WIN ** order
    y = v.reshape(B, H // side, side, W // side, side, v.shape[3], R)
    m = y.mean(axis=(2, 4), keepdims=True)
    return np.broadcast_to(m, y.shape).reshape(v.shape)


def setup_inputs():
    s = mx_kscale(E)
    return {"x": bf(np.random.standard_normal((B, H, W, L, R)) * s.reshape(L, R)),
            "w1": bf(np.random.standard_normal((E, F)) / np.sqrt(E) / s[:, None]),
            "b1": bf(np.random.standard_normal(F) * 0.1),
            "w2": bf(np.random.standard_normal((F, R)) * 2.0 / np.sqrt(F)),
            "b2": bf(np.random.standard_normal(R) * 0.1)}


def reference(x, w1, b1, w2, b2):
    x = f64(x)
    w1q = mxq(f64(w1), 0, "e4m3")
    w2q = mxq(f64(w2), 0, "e4m3")
    outs = []
    for i in range(L):
        upper = x[:, :, :, i:, :]
        if i == 0:
            merged = upper.reshape(P, E)
        else:
            lower = avg_siblings(x[:, :, :, :i, :], i)
            merged = np.concatenate([lower, upper], axis=3).reshape(P, E)
        hid = new_gelu((mxq(merged, 1, "e4m3") @ w1q) + f64(b1))
        outs.append((mxq(hid, 1, "e4m3") @ w2q) + f64(b2))
    return np.stack(outs, axis=1).reshape(B, H, W, L, R)

@@ -1,0 +1,222 @@
+from contextlib import ExitStack
+
+import concourse.masks as masks
+import concourse.mybir as mybir
+
+F32 = mybir.dt.float32
+BF16 = mybir.dt.bfloat16
+U32 = mybir.dt.uint32
+U8 = mybir.dt.uint8
+FP8X4 = mybir.dt.float8_e4m3fn_x4
+ACT = mybir.ActivationFunctionType
+ALU = mybir.AluOpType
+AXIS = mybir.AxisListType
+
+P = 128
+PACK = 4
+K_PASS = P * PACK
+LEVELS = 2
+R = 512
+F = 512
+WINDOW_ROWS = 8
+WINDOW_COLS = 4
+BANKS = 8
+
+VECTOR_COLS = 320
+
+FLOPS = 2 * LEVELS * P * (LEVELS * R * F + F * R)
+
+
+def regroup(copy, grouped, rows):
+    copy(
+        out=grouped.rearrange("p (g i) t -> p g t i", i=4),
+        in_=rows.rearrange("p t (g i) -> p g t i", i=4),
+    )
+
+
+def tile_treemlpv3_pa_s_kernel(tc, x, w1, b1, w2, b2, out):
+    nc = tc.nc
+    vector_share = slice(0, VECTOR_COLS)
+    scalar_share = slice(VECTOR_COLS, F)
+
+    with ExitStack() as ctx:
+        sbuf = ctx.enter_context(tc.tile_pool(name="sbuf", bufs=1))
+        psum = ctx.enter_context(tc.psum_pool(name="psum", bufs=1))
+        ctx.enter_context(tc.manual_schedule())
+
+        def bank(n, shape, dtype, name):
+            return psum.tile(shape, dtype, name=name, tag="bank%d" % n)
+
+        x_sb = sbuf.tile([P, LEVELS * R], BF16)
+        nc.sync.dma_start(out=x_sb[:], in_=x.rearrange("b h w l r -> (b h w) (l r)"))
+        w1_rows = sbuf.tile([P, LEVELS, PACK, F], BF16)
+        for c in range(LEVELS):
+            nc.sync.dma_start(
+                out=w1_rows[:, c],
+                in_=w1[c * K_PASS : (c + 1) * K_PASS, :].rearrange("(p t) f -> p t f", t=PACK),
+            )
+        w2_rows = sbuf.tile([P, PACK, R], BF16)
+        nc.sync.dma_start(out=w2_rows[:], in_=w2.rearrange("(t p) r -> p t r", p=P))
+
+        bias_rows = sbuf.tile([P, R + P], BF16)
+        nc.vector.memset(bias_rows[:], 0.0)
+        nc.scalar.dma_start(out=bias_rows[0:1, 0:R], in_=b2.rearrange("(o r) -> o r", o=1))
+        nc.scalar.dma_start(
+            out=bias_rows[0:PACK, R : R + P], in_=b1.rearrange("(j p) -> j p", p=P)
+        )
+        ones = sbuf.tile([P, P], BF16)
+        nc.vector.memset(ones[:], 1.0)
+        table_in = sbuf.tile([P, 1], F32)
+        nc.vector.memset(table_in[:], 0.0)
+        table_out = sbuf.tile([P, 1], F32)
+        nc.scalar.activation(out=table_out[:], in_=table_in[:], func=ACT.Gelu_apprx_tanh)
+
+        ident = sbuf.tile([P, P], F32)
+        masks.make_identity(nc, ident[:])
+        ident_bf = sbuf.tile([P, P], BF16)
+        nc.vector.tensor_copy(out=ident_bf[:], in_=ident[:])
+        in_window = sbuf.tile([P, WINDOW_ROWS, WINDOW_COLS], F32)
+        nc.vector.tensor_reduce(
+            out=in_window[:],
+            in_=ident[:].rearrange("p (a h c w) -> p a c h w", a=WINDOW_ROWS, h=2, w=2),
+            axis=AXIS.XY,
+            op=ALU.add,
+        )
+        same_window = sbuf.tile([P, P], BF16)
+        nc.vector.tensor_copy(
+            out=same_window[:].rearrange("p (a h c w) -> p a h c w", a=WINDOW_ROWS, h=2, w=2),
+            in_=in_window[:]
+            .unsqueeze(2)
+            .unsqueeze(4)
+            .to_broadcast([P, WINDOW_ROWS, 2, WINDOW_COLS, 2]),
+        )
+
+        x_words = x_sb[:].bitcast(F32).rearrange("r (c p u) -> r c u p", c=LEVELS, u=2)
+        xT = bank(0, [P, LEVELS, 2, P], F32, "xT")
+        for c in range(LEVELS):
+            for u in range(2):
+                nc.tensor.transpose(xT[:, c, u, :], x_words[:, c, u, :], ident[:])
+        x_level0 = x_sb[:, 0:R].rearrange("r (p t) -> r t p", t=PACK)
+        sumT = bank(1, [P, PACK, P], F32, "sumT")
+        for t in range(PACK):
+            nc.tensor.matmul(
+                sumT[:, t, :], lhsT=x_level0[:, t, :], rhs=same_window[:], start=True, stop=True
+            )
+        bias_ps = bank(3, [P, R + P], BF16, "bias_ps")
+        nc.tensor.matmul(bias_ps[:, 0:R], lhsT=ones[:], rhs=bias_rows[:, 0:R], start=True, stop=True)
+        nc.tensor.transpose(bias_ps[:, R : R + P], bias_rows[:, R : R + P], ident_bf[:])
+
+        X0, X1, MEAN0 = 0, 1, 2
+        m_codes = sbuf.tile([P, 3, P], U32, align_bytes=64)
+        m_scales = sbuf.tile([P, 3, P], U8, align_bytes=64)
+        w1_grouped = sbuf.tile([P, LEVELS, F, PACK], BF16, align_bytes=64)
+        w1_codes = sbuf.tile([P, LEVELS, F], U32, align_bytes=64)
+        w1_scales = sbuf.tile([P, LEVELS, F], U8, align_bytes=64)
+
+        def regroup_w1(c):
+            regroup(nc.vector.tensor_copy, w1_grouped[:, c, vector_share, :], w1_rows[:, c, :, vector_share])
+            regroup(nc.scalar.copy, w1_grouped[:, c, scalar_share, :], w1_rows[:, c, :, scalar_share])
+
+        def quantise_w1(c):
+            nc.vector.quantize_mx(
+                out=w1_codes[:, c, :].bitcast(FP8X4),
+                scales=w1_scales[:, c, :],
+                in_=w1_grouped[:, c].rearrange("p f t -> p (f t)"),
+            )
+
+        x_grouped = sbuf.tile([P, LEVELS * P * PACK], BF16, align_bytes=64)
+        nc.scalar.copy(
+            out=x_grouped[:].bitcast(F32).rearrange("p (c r u) -> p c r u", c=LEVELS, u=2),
+            in_=xT[:].rearrange("p c u r -> p c r u"),
+        )
+        regroup_w1(0)
+        nc.vector.quantize_mx(
+            out=m_codes[:, X0 : X1 + 1, :].rearrange("p b r -> p (b r)").bitcast(FP8X4),
+            scales=m_scales[:, X0 : X1 + 1, :].rearrange("p b r -> p (b r)"),
+            in_=x_grouped[:],
+        )
+        mean_grouped = sbuf.tile([P, P, PACK], BF16, align_bytes=64)
+        nc.scalar.mul(out=mean_grouped[:], in_=sumT[:].rearrange("p t r -> p r t"), mul=0.25)
+        regroup_w1(1)
+        bias_sb = sbuf.tile([P, R + PACK], BF16)
+        nc.scalar.copy(out=bias_sb[:], in_=bias_ps[:, 0 : R + PACK])
+
+        hid_acc = [
+            [
+                bank((BANKS // 2 + PACK * i + j) % BANKS, [P, P], F32, "hid_acc_%d_%d" % (i, j))
+                for j in range(PACK)
+            ]
+            for i in range(LEVELS)
+        ]
+
+        def first_product(c):
+            for i in range(LEVELS):
+                block = X1 if c == 1 else (X0 if i == 0 else MEAN0)
+                for j in range(PACK):
+                    chunk = slice(j * P, (j + 1) * P)
+                    nc.tensor.matmul_mx(
+                        out=hid_acc[i][j][:],
+                        lhsT=w1_codes[:, c, chunk].bitcast(FP8X4),
+                        lhsT_scale=w1_scales[:, c, chunk],
+                        rhs=m_codes[:, block, :].bitcast(FP8X4),
+                        rhs_scale=m_scales[:, block, :],
+                        start=(c == 0),
+                        stop=(c == LEVELS - 1),
+                    )
+
+        quantise_w1(0)
+        nc.vector.quantize_mx(
+            out=m_codes[:, MEAN0, :].bitcast(FP8X4),
+            scales=m_scales[:, MEAN0, :],
+            in_=mean_grouped[:].rearrange("p r t -> p (r t)"),
+        )
+        first_product(0)
+        quantise_w1(1)
+        first_product(1)
+
+        w2_grouped = sbuf.tile([P, R, PACK], BF16, align_bytes=64)
+        w2_codes = sbuf.tile([P, R], U32, align_bytes=64)
+        w2_scales = sbuf.tile([P, R], U8, align_bytes=64)
+        regroup(nc.vector.tensor_copy, w2_grouped[:, vector_share, :], w2_rows[:, :, vector_share])
+        regroup(nc.scalar.copy, w2_grouped[:, scalar_share, :], w2_rows[:, :, scalar_share])
+        nc.vector.quantize_mx(
+            out=w2_codes[:].bitcast(FP8X4),
+            scales=w2_scales[:],
+            in_=w2_grouped[:].rearrange("p r t -> p (r t)"),
+        )
+
+        out_acc = []
+        for i in range(LEVELS):
+            hid_rows = sbuf.tile([P, PACK, P], BF16, name="hid_rows_%d" % i)
+            for j in range(PACK):
+                nc.scalar.activation(
+                    out=hid_rows[:, j, :],
+                    in_=hid_acc[i][j][:],
+                    func=ACT.Gelu_apprx_tanh,
+                    bias=bias_sb[:, R + j : R + j + 1],
+                )
+            hid_grouped = sbuf.tile([P, P, PACK], BF16, name="hid_grouped_%d" % i, align_bytes=64)
+            regroup(nc.vector.tensor_copy, hid_grouped[:], hid_rows[:])
+            hid_codes = sbuf.tile([P, P], U32, name="hid_codes_%d" % i, align_bytes=64)
+            hid_scales = sbuf.tile([P, P], U8, name="hid_scales_%d" % i, align_bytes=64)
+            nc.vector.quantize_mx(
+                out=hid_codes[:].bitcast(FP8X4),
+                scales=hid_scales[:],
+                in_=hid_grouped[:].rearrange("p r t -> p (r t)"),
+            )
+            out_acc.append(bank(BANKS // 2 + i, [P, R], F32, "out_acc_%d" % i))
+            nc.tensor.matmul_mx(
+                out=out_acc[i][:],
+                lhsT=hid_codes[:].bitcast(FP8X4),
+                lhsT_scale=hid_scales[:],
+                rhs=w2_codes[:].bitcast(FP8X4),
+                rhs_scale=w2_scales[:],
+                start=True,
+                stop=True,
+            )
+
+        out_rows = out.rearrange("b h w l r -> (b h w) l r")
+        for i in range(LEVELS):
+            result = sbuf.tile([P, R], F32, name="result_%d" % i)
+            nc.vector.tensor_tensor(out=result[:], in0=out_acc[i][:], in1=bias_sb[:, 0:R], op=ALU.add)
+            nc.sync.dma_start(out=out_rows[:, i, :], in_=result[:])

@@ -22,7 +22,8 @@ WINDOW_ROWS = 8
 WINDOW_COLS = 4
 BANKS = 8
 
-VECTOR_COLS = 320
+CHUNK = 256
+VECTOR_COLS = 128
 
 FLOPS = 2 * LEVELS * P * (LEVELS * R * F + F * R)
 
@@ -36,8 +37,6 @@ def regroup(copy, grouped, rows):
 
 def tile_treemlpv3_pa_s_kernel(tc, x, w1, b1, w2, b2, out):
     nc = tc.nc
-    vector_share = slice(0, VECTOR_COLS)
-    scalar_share = slice(VECTOR_COLS, F)
 
     with ExitStack() as ctx:
         sbuf = ctx.enter_context(tc.tile_pool(name="sbuf", bufs=1))
@@ -47,34 +46,33 @@ def tile_treemlpv3_pa_s_kernel(tc, x, w1, b1, w2, b2, out):
         def bank(n, shape, dtype, name):
             return psum.tile(shape, dtype, name=name, tag="bank%d" % n)
 
-        x_sb = sbuf.tile([P, LEVELS * R], BF16)
-        nc.sync.dma_start(out=x_sb[:], in_=x.rearrange("b h w l r -> (b h w) (l r)"))
+        table_in = sbuf.tile([P, 1], F32)
+        nc.vector.memset(table_in[:], 0.0)
+        table_out = sbuf.tile([P, 1], F32)
+        nc.scalar.activation(out=table_out[:], in_=table_in[:], func=ACT.Gelu_apprx_tanh)
+        bias_rows = sbuf.tile([P, P], BF16)
+        nc.vector.memset(bias_rows[:].bitcast(F32), 0.0)
+
+        x_rows = x.rearrange("b h w l r -> (b h w) l r")
+        x_sb = sbuf.tile([P, LEVELS, R], BF16)
         w1_rows = sbuf.tile([P, LEVELS, PACK, F], BF16)
         for c in range(LEVELS):
+            nc.sync.dma_start(out=x_sb[:, c, :], in_=x_rows[:, c, :])
+            if c == 0:
+                nc.sync.dma_start(
+                    out=bias_rows[0:PACK, :], in_=b1.rearrange("(j p) -> j p", p=P)
+                )
             nc.sync.dma_start(
                 out=w1_rows[:, c],
                 in_=w1[c * K_PASS : (c + 1) * K_PASS, :].rearrange("(p t) f -> p t f", t=PACK),
             )
         w2_rows = sbuf.tile([P, PACK, R], BF16)
         nc.sync.dma_start(out=w2_rows[:], in_=w2.rearrange("(t p) r -> p t r", p=P))
-
-        bias_rows = sbuf.tile([P, R + P], BF16)
-        nc.vector.memset(bias_rows[:], 0.0)
-        nc.scalar.dma_start(out=bias_rows[0:1, 0:R], in_=b2.rearrange("(o r) -> o r", o=1))
-        nc.scalar.dma_start(
-            out=bias_rows[0:PACK, R : R + P], in_=b1.rearrange("(j p) -> j p", p=P)
-        )
-        ones = sbuf.tile([P, P], BF16)
-        nc.vector.memset(ones[:], 1.0)
-        table_in = sbuf.tile([P, 1], F32)
-        nc.vector.memset(table_in[:], 0.0)
-        table_out = sbuf.tile([P, 1], F32)
-        nc.scalar.activation(out=table_out[:], in_=table_in[:], func=ACT.Gelu_apprx_tanh)
+        b2_sb = sbuf.tile([P, R], BF16)
+        nc.sync.dma_start(out=b2_sb[:], in_=b2.partition_broadcast(P))
 
         ident = sbuf.tile([P, P], F32)
         masks.make_identity(nc, ident[:])
-        ident_bf = sbuf.tile([P, P], BF16)
-        nc.vector.tensor_copy(out=ident_bf[:], in_=ident[:])
         in_window = sbuf.tile([P, WINDOW_ROWS, WINDOW_COLS], F32)
         nc.vector.tensor_reduce(
             out=in_window[:],
@@ -82,64 +80,82 @@ def tile_treemlpv3_pa_s_kernel(tc, x, w1, b1, w2, b2, out):
             axis=AXIS.XY,
             op=ALU.add,
         )
-        same_window = sbuf.tile([P, P], BF16)
+        quarter = sbuf.tile([P, WINDOW_ROWS, WINDOW_COLS], F32)
+        nc.vector.tensor_scalar_mul(out=quarter[:], in0=in_window[:], scalar1=0.25)
+        mean_of = sbuf.tile([P, P], BF16)
         nc.vector.tensor_copy(
-            out=same_window[:].rearrange("p (a h c w) -> p a h c w", a=WINDOW_ROWS, h=2, w=2),
-            in_=in_window[:]
+            out=mean_of[:].rearrange("p (a h c w) -> p a h c w", a=WINDOW_ROWS, h=2, w=2),
+            in_=quarter[:]
             .unsqueeze(2)
             .unsqueeze(4)
             .to_broadcast([P, WINDOW_ROWS, 2, WINDOW_COLS, 2]),
         )
+        ident_bf = sbuf.tile([P, P], BF16)
+        nc.vector.tensor_copy(out=ident_bf[:], in_=ident[:])
 
-        x_words = x_sb[:].bitcast(F32).rearrange("r (c p u) -> r c u p", c=LEVELS, u=2)
-        xT = bank(0, [P, LEVELS, 2, P], F32, "xT")
-        for c in range(LEVELS):
+        x_words = (
+            x_sb[:].rearrange("r c k -> r (c k)").bitcast(F32).rearrange(
+                "r (c p u) -> r c u p", c=LEVELS, u=2
+            )
+        )
+        xT = [bank(c, [P, 2, P], F32, "xT_%d" % c) for c in range(LEVELS)]
+
+        def transpose_x(c):
             for u in range(2):
-                nc.tensor.transpose(xT[:, c, u, :], x_words[:, c, u, :], ident[:])
-        x_level0 = x_sb[:, 0:R].rearrange("r (p t) -> r t p", t=PACK)
-        sumT = bank(1, [P, PACK, P], F32, "sumT")
+                nc.tensor.transpose(xT[c][:, u, :], x_words[:, c, u, :], ident[:])
+
+        transpose_x(0)
+        x_level0 = x_sb[:, 0, :].rearrange("r (p t) -> r t p", t=PACK)
+        meanT = bank(2, [P, PACK, P], BF16, "meanT")
         for t in range(PACK):
             nc.tensor.matmul(
-                sumT[:, t, :], lhsT=x_level0[:, t, :], rhs=same_window[:], start=True, stop=True
+                meanT[:, t, :], lhsT=x_level0[:, t, :], rhs=mean_of[:], start=True, stop=True
             )
-        bias_ps = bank(3, [P, R + P], BF16, "bias_ps")
-        nc.tensor.matmul(bias_ps[:, 0:R], lhsT=ones[:], rhs=bias_rows[:, 0:R], start=True, stop=True)
-        nc.tensor.transpose(bias_ps[:, R : R + P], bias_rows[:, R : R + P], ident_bf[:])
+        biasT = bank(3, [P, P], BF16, "biasT")
+        nc.tensor.transpose(biasT[:], bias_rows[:], ident_bf[:])
+        transpose_x(1)
 
         X0, X1, MEAN0 = 0, 1, 2
+        m_grouped = sbuf.tile([P, 3, P * PACK], BF16, align_bytes=64)
         m_codes = sbuf.tile([P, 3, P], U32, align_bytes=64)
         m_scales = sbuf.tile([P, 3, P], U8, align_bytes=64)
         w1_grouped = sbuf.tile([P, LEVELS, F, PACK], BF16, align_bytes=64)
         w1_codes = sbuf.tile([P, LEVELS, F], U32, align_bytes=64)
         w1_scales = sbuf.tile([P, LEVELS, F], U8, align_bytes=64)
+        w2_grouped = sbuf.tile([P, R, PACK], BF16, align_bytes=64)
+        w2_codes = sbuf.tile([P, R], U32, align_bytes=64)
+        w2_scales = sbuf.tile([P, R], U8, align_bytes=64)
 
-        def regroup_w1(c):
-            regroup(nc.vector.tensor_copy, w1_grouped[:, c, vector_share, :], w1_rows[:, c, :, vector_share])
-            regroup(nc.scalar.copy, w1_grouped[:, c, scalar_share, :], w1_rows[:, c, :, scalar_share])
+        def regroup_chunk(grouped, rows, n, vector_cols):
+            cut = n * CHUNK + vector_cols
+            vector_share = slice(n * CHUNK, cut)
+            scalar_share = slice(cut, (n + 1) * CHUNK)
+            regroup(nc.vector.tensor_copy, grouped[:, vector_share, :], rows[:, :, vector_share])
+            regroup(nc.scalar.copy, grouped[:, scalar_share, :], rows[:, :, scalar_share])
 
-        def quantise_w1(c):
+        def quantise_chunk(codes, scales, grouped, n):
+            cols = slice(n * CHUNK, (n + 1) * CHUNK)
             nc.vector.quantize_mx(
-                out=w1_codes[:, c, :].bitcast(FP8X4),
-                scales=w1_scales[:, c, :],
-                in_=w1_grouped[:, c].rearrange("p f t -> p (f t)"),
+                out=codes[:, cols].bitcast(FP8X4),
+                scales=scales[:, cols],
+                in_=grouped[:, cols, :].rearrange("p f t -> p (f t)"),
             )
 
-        x_grouped = sbuf.tile([P, LEVELS * P * PACK], BF16, align_bytes=64)
-        nc.scalar.copy(
-            out=x_grouped[:].bitcast(F32).rearrange("p (c r u) -> p c r u", c=LEVELS, u=2),
-            in_=xT[:].rearrange("p c u r -> p c r u"),
-        )
-        regroup_w1(0)
-        nc.vector.quantize_mx(
-            out=m_codes[:, X0 : X1 + 1, :].rearrange("p b r -> p (b r)").bitcast(FP8X4),
-            scales=m_scales[:, X0 : X1 + 1, :].rearrange("p b r -> p (b r)"),
-            in_=x_grouped[:],
-        )
-        mean_grouped = sbuf.tile([P, P, PACK], BF16, align_bytes=64)
-        nc.scalar.mul(out=mean_grouped[:], in_=sumT[:].rearrange("p t r -> p r t"), mul=0.25)
-        regroup_w1(1)
-        bias_sb = sbuf.tile([P, R + PACK], BF16)
-        nc.scalar.copy(out=bias_sb[:], in_=bias_ps[:, 0 : R + PACK])
+        def copy_xT(copy, c):
+            copy(
+                out=m_grouped[:, X0 + c, :].bitcast(F32).rearrange("p (r u) -> p r u", u=2),
+                in_=xT[c][:].rearrange("p u r -> p r u"),
+            )
+
+        def quantise_merged(b):
+            nc.vector.quantize_mx(
+                out=m_codes[:, b, :].bitcast(FP8X4), scales=m_scales[:, b, :], in_=m_grouped[:, b, :]
+            )
+
+        copy_xT(nc.vector.tensor_copy, 0)
+        quantise_merged(X0)
+        b1_sb = sbuf.tile([P, PACK], BF16)
+        nc.scalar.copy(out=b1_sb[:], in_=biasT[:, 0:PACK])
 
         hid_acc = [
             [
@@ -149,74 +165,95 @@ def tile_treemlpv3_pa_s_kernel(tc, x, w1, b1, w2, b2, out):
             for i in range(LEVELS)
         ]
 
-        def first_product(c):
-            for i in range(LEVELS):
-                block = X1 if c == 1 else (X0 if i == 0 else MEAN0)
-                for j in range(PACK):
-                    chunk = slice(j * P, (j + 1) * P)
-                    nc.tensor.matmul_mx(
-                        out=hid_acc[i][j][:],
-                        lhsT=w1_codes[:, c, chunk].bitcast(FP8X4),
-                        lhsT_scale=w1_scales[:, c, chunk],
-                        rhs=m_codes[:, block, :].bitcast(FP8X4),
-                        rhs_scale=m_scales[:, block, :],
-                        start=(c == 0),
-                        stop=(c == LEVELS - 1),
-                    )
+        def first_product(c, i, js):
+            block = X1 if c == 1 else (X0 if i == 0 else MEAN0)
+            for j in js:
+                chunk = slice(j * P, (j + 1) * P)
+                nc.tensor.matmul_mx(
+                    out=hid_acc[i][j][:],
+                    lhsT=w1_codes[:, c, chunk].bitcast(FP8X4),
+                    lhsT_scale=w1_scales[:, c, chunk],
+                    rhs=m_codes[:, block, :].bitcast(FP8X4),
+                    rhs_scale=m_scales[:, block, :],
+                    start=(c == 0),
+                    stop=(c == LEVELS - 1),
+                )
 
-        quantise_w1(0)
-        nc.vector.quantize_mx(
-            out=m_codes[:, MEAN0, :].bitcast(FP8X4),
-            scales=m_scales[:, MEAN0, :],
-            in_=mean_grouped[:].rearrange("p r t -> p (r t)"),
+        regroup_chunk(w1_grouped[:, 0], w1_rows[:, 0], 0, VECTOR_COLS)
+        regroup_chunk(w1_grouped[:, 0], w1_rows[:, 0], 1, VECTOR_COLS)
+        nc.scalar.copy(
+            out=m_grouped[:, MEAN0, :].rearrange("p (r t) -> p r t", t=PACK),
+            in_=meanT[:].rearrange("p t r -> p r t"),
         )
-        first_product(0)
-        quantise_w1(1)
-        first_product(1)
+        quantise_chunk(w1_codes[:, 0], w1_scales[:, 0], w1_grouped[:, 0], 0)
+        copy_xT(nc.vector.tensor_copy, 1)
+        quantise_chunk(w1_codes[:, 0], w1_scales[:, 0], w1_grouped[:, 0], 1)
+        first_product(0, 0, range(0, 2))
+        first_product(0, 0, range(2, 4))
+        regroup_chunk(w1_grouped[:, 1], w1_rows[:, 1], 0, VECTOR_COLS)
+        regroup_chunk(w1_grouped[:, 1], w1_rows[:, 1], 1, VECTOR_COLS)
+        quantise_merged(X1)
+        quantise_merged(MEAN0)
+        first_product(0, 1, range(0, 4))
+        quantise_chunk(w1_codes[:, 1], w1_scales[:, 1], w1_grouped[:, 1], 0)
+        quantise_chunk(w1_codes[:, 1], w1_scales[:, 1], w1_grouped[:, 1], 1)
+        first_product(1, 0, range(0, 2))
+        first_product(1, 0, range(2, 4))
+        first_product(1, 1, range(0, 4))
 
-        w2_grouped = sbuf.tile([P, R, PACK], BF16, align_bytes=64)
-        w2_codes = sbuf.tile([P, R], U32, align_bytes=64)
-        w2_scales = sbuf.tile([P, R], U8, align_bytes=64)
-        regroup(nc.vector.tensor_copy, w2_grouped[:, vector_share, :], w2_rows[:, :, vector_share])
-        regroup(nc.scalar.copy, w2_grouped[:, scalar_share, :], w2_rows[:, :, scalar_share])
-        nc.vector.quantize_mx(
-            out=w2_codes[:].bitcast(FP8X4),
-            scales=w2_scales[:],
-            in_=w2_grouped[:].rearrange("p r t -> p (r t)"),
-        )
+        hid_rows = [sbuf.tile([P, PACK, P], BF16, name="hid_rows_%d" % i) for i in range(LEVELS)]
+        hid_grouped = [
+            sbuf.tile([P, P, PACK], BF16, name="hid_grouped_%d" % i, align_bytes=64)
+            for i in range(LEVELS)
+        ]
+        hid_codes = [
+            sbuf.tile([P, P], U32, name="hid_codes_%d" % i, align_bytes=64) for i in range(LEVELS)
+        ]
+        hid_scales = [
+            sbuf.tile([P, P], U8, name="hid_scales_%d" % i, align_bytes=64) for i in range(LEVELS)
+        ]
 
-        out_acc = []
-        for i in range(LEVELS):
-            hid_rows = sbuf.tile([P, PACK, P], BF16, name="hid_rows_%d" % i)
+        def gelu(i):
             for j in range(PACK):
                 nc.scalar.activation(
-                    out=hid_rows[:, j, :],
+                    out=hid_rows[i][:, j, :],
                     in_=hid_acc[i][j][:],
                     func=ACT.Gelu_apprx_tanh,
-                    bias=bias_sb[:, R + j : R + j + 1],
+                    bias=b1_sb[:, j : j + 1],
                 )
-            hid_grouped = sbuf.tile([P, P, PACK], BF16, name="hid_grouped_%d" % i, align_bytes=64)
-            regroup(nc.vector.tensor_copy, hid_grouped[:], hid_rows[:])
-            hid_codes = sbuf.tile([P, P], U32, name="hid_codes_%d" % i, align_bytes=64)
-            hid_scales = sbuf.tile([P, P], U8, name="hid_scales_%d" % i, align_bytes=64)
+
+        def quantise_hid(i):
             nc.vector.quantize_mx(
-                out=hid_codes[:].bitcast(FP8X4),
-                scales=hid_scales[:],
-                in_=hid_grouped[:].rearrange("p r t -> p (r t)"),
+                out=hid_codes[i][:].bitcast(FP8X4),
+                scales=hid_scales[i][:],
+                in_=hid_grouped[i][:].rearrange("p r t -> p (r t)"),
             )
-            out_acc.append(bank(BANKS // 2 + i, [P, R], F32, "out_acc_%d" % i))
-            nc.tensor.matmul_mx(
-                out=out_acc[i][:],
-                lhsT=hid_codes[:].bitcast(FP8X4),
-                lhsT_scale=hid_scales[:],
-                rhs=w2_codes[:].bitcast(FP8X4),
-                rhs_scale=w2_scales[:],
-                start=True,
-                stop=True,
-            )
+
+        regroup_chunk(w2_grouped, w2_rows, 0, VECTOR_COLS)
+        gelu(0)
+        regroup_chunk(w2_grouped, w2_rows, 1, VECTOR_COLS)
+        gelu(1)
+        quantise_chunk(w2_codes, w2_scales, w2_grouped, 0)
+        regroup(nc.vector.tensor_copy, hid_grouped[0][:], hid_rows[0][:])
+        quantise_chunk(w2_codes, w2_scales, w2_grouped, 1)
+        quantise_hid(0)
+        regroup(nc.vector.tensor_copy, hid_grouped[1][:], hid_rows[1][:])
+        quantise_hid(1)
 
         out_rows = out.rearrange("b h w l r -> (b h w) l r")
         for i in range(LEVELS):
-            result = sbuf.tile([P, R], F32, name="result_%d" % i)
-            nc.vector.tensor_tensor(out=result[:], in0=out_acc[i][:], in1=bias_sb[:, 0:R], op=ALU.add)
-            nc.sync.dma_start(out=out_rows[:, i, :], in_=result[:])
+            for n in range(R // CHUNK):
+                cols = slice(n * CHUNK, (n + 1) * CHUNK)
+                out_acc = bank(BANKS // 2 + 2 * i + n, [P, CHUNK], F32, "out_acc_%d_%d" % (i, n))
+                nc.tensor.matmul_mx(
+                    out=out_acc[:],
+                    lhsT=hid_codes[i][:].bitcast(FP8X4),
+                    lhsT_scale=hid_scales[i][:],
+                    rhs=w2_codes[:, cols].bitcast(FP8X4),
+                    rhs_scale=w2_scales[:, cols],
+                    start=True,
+                    stop=True,
+                )
+                result = sbuf.tile([P, CHUNK], F32, name="result_%d_%d" % (i, n))
+                nc.vector.tensor_tensor(out=result[:], in0=out_acc[:], in1=b2_sb[:, cols], op=ALU.add)
+                nc.sync.dma_start(out=out_rows[:, i, cols], in_=result[:])

@@ -23,7 +23,7 @@ WINDOW_COLS = 4
 BANKS = 8
 
 CHUNK = 256
-VECTOR_COLS = 128
+VECTOR_COLS = 192
 
 FLOPS = 2 * LEVELS * P * (LEVELS * R * F + F * R)
 

@@ -104,6 +104,9 @@ def tile_treemlpv3_pa_s_kernel(tc, x, w1, b1, w2, b2, out):
             for u in range(2):
                 nc.tensor.transpose(xT[c][:, u, :], x_words[:, c, u, :], ident[:])
 
+        warm_up = bank(3, [P, P], F32, "warm_up_0")
+        for n in range(3):
+            nc.tensor.matmul(warm_up[:], lhsT=ident[:], rhs=ident[:], start=True, stop=True)
         transpose_x(0)
         x_level0 = x_sb[:, 0, :].rearrange("r (p t) -> r t p", t=PACK)
         meanT = bank(2, [P, PACK, P], BF16, "meanT")
@@ -113,7 +116,6 @@ def tile_treemlpv3_pa_s_kernel(tc, x, w1, b1, w2, b2, out):
             )
         biasT = bank(3, [P, P], BF16, "biasT")
         nc.tensor.transpose(biasT[:], bias_rows[:], ident_bf[:])
-        transpose_x(1)
 
         X0, X1, MEAN0 = 0, 1, 2
         m_grouped = sbuf.tile([P, 3, P * PACK], BF16, align_bytes=64)
@@ -157,20 +159,21 @@ def tile_treemlpv3_pa_s_kernel(tc, x, w1, b1, w2, b2, out):
         b1_sb = sbuf.tile([P, PACK], BF16)
         nc.scalar.copy(out=b1_sb[:], in_=biasT[:, 0:PACK])
 
-        hid_acc = [
-            [
-                bank((BANKS // 2 + PACK * i + j) % BANKS, [P, P], F32, "hid_acc_%d_%d" % (i, j))
-                for j in range(PACK)
-            ]
-            for i in range(LEVELS)
-        ]
+        hid_acc = {}
+
+        def open_level(i):
+            for j in range(PACK):
+                n = (BANKS // 2 + PACK * i + j) % BANKS
+                hid_acc[i, j] = bank(n, [P, P], F32, "hid_acc_%d_%d" % (i, j))
+
+        open_level(0)
 
         def first_product(c, i, js):
             block = X1 if c == 1 else (X0 if i == 0 else MEAN0)
             for j in js:
                 chunk = slice(j * P, (j + 1) * P)
                 nc.tensor.matmul_mx(
-                    out=hid_acc[i][j][:],
+                    out=hid_acc[i, j][:],
                     lhsT=w1_codes[:, c, chunk].bitcast(FP8X4),
                     lhsT_scale=w1_scales[:, c, chunk],
                     rhs=m_codes[:, block, :].bitcast(FP8X4),
@@ -186,14 +189,32 @@ def tile_treemlpv3_pa_s_kernel(tc, x, w1, b1, w2, b2, out):
             in_=meanT[:].rearrange("p t r -> p r t"),
         )
         quantise_chunk(w1_codes[:, 0], w1_scales[:, 0], w1_grouped[:, 0], 0)
-        copy_xT(nc.vector.tensor_copy, 1)
         quantise_chunk(w1_codes[:, 0], w1_scales[:, 0], w1_grouped[:, 0], 1)
+        quantise_merged(MEAN0)
+
+        def keep_warm(n, passes):
+            spare = bank(3, [P, P], F32, "spare_%d" % n)
+            for k in range(passes):
+                nc.tensor.matmul_mx(
+                    out=spare[:],
+                    lhsT=m_codes[:, X0, :].bitcast(FP8X4),
+                    lhsT_scale=m_scales[:, X0, :],
+                    rhs=m_codes[:, X0, :].bitcast(FP8X4),
+                    rhs_scale=m_scales[:, X0, :],
+                    start=True,
+                    stop=True,
+                )
+
+        keep_warm(0, 6)
+        transpose_x(1)
         first_product(0, 0, range(0, 2))
         first_product(0, 0, range(2, 4))
+        keep_warm(1, 4)
+        copy_xT(nc.scalar.copy, 1)
         regroup_chunk(w1_grouped[:, 1], w1_rows[:, 1], 0, VECTOR_COLS)
         regroup_chunk(w1_grouped[:, 1], w1_rows[:, 1], 1, VECTOR_COLS)
         quantise_merged(X1)
-        quantise_merged(MEAN0)
+        open_level(1)
         first_product(0, 1, range(0, 4))
         quantise_chunk(w1_codes[:, 1], w1_scales[:, 1], w1_grouped[:, 1], 0)
         quantise_chunk(w1_codes[:, 1], w1_scales[:, 1], w1_grouped[:, 1], 1)
@@ -217,7 +238,7 @@ def tile_treemlpv3_pa_s_kernel(tc, x, w1, b1, w2, b2, out):
             for j in range(PACK):
                 nc.scalar.activation(
                     out=hid_rows[i][:, j, :],
-                    in_=hid_acc[i][j][:],
+                    in_=hid_acc[i, j][:],
                     func=ACT.Gelu_apprx_tanh,
                     bias=b1_sb[:, j : j + 1],
                 )

@@ -23,7 +23,7 @@ WINDOW_COLS = 4
 BANKS = 8
 
 CHUNK = 256
-VECTOR_COLS = 192
+VECTOR_COLS = 160
 
 FLOPS = 2 * LEVELS * P * (LEVELS * R * F + F * R)
 
@@ -50,24 +50,19 @@ def tile_treemlpv3_pa_s_kernel(tc, x, w1, b1, w2, b2, out):
         nc.vector.memset(table_in[:], 0.0)
         table_out = sbuf.tile([P, 1], F32)
         nc.scalar.activation(out=table_out[:], in_=table_in[:], func=ACT.Gelu_apprx_tanh)
-        bias_rows = sbuf.tile([P, P], BF16)
-        nc.vector.memset(bias_rows[:].bitcast(F32), 0.0)
 
-        x_rows = x.rearrange("b h w l r -> (b h w) l r")
-        x_sb = sbuf.tile([P, LEVELS, R], BF16)
+        x_sb = sbuf.tile([P, LEVELS * R], BF16)
+        nc.sync.dma_start(out=x_sb[:], in_=x.rearrange("b h w l r -> (b h w) (l r)"))
         w1_rows = sbuf.tile([P, LEVELS, PACK, F], BF16)
         for c in range(LEVELS):
-            nc.sync.dma_start(out=x_sb[:, c, :], in_=x_rows[:, c, :])
-            if c == 0:
-                nc.sync.dma_start(
-                    out=bias_rows[0:PACK, :], in_=b1.rearrange("(j p) -> j p", p=P)
-                )
             nc.sync.dma_start(
                 out=w1_rows[:, c],
                 in_=w1[c * K_PASS : (c + 1) * K_PASS, :].rearrange("(p t) f -> p t f", t=PACK),
             )
+        b1_sb = sbuf.tile([P, PACK], BF16)
+        nc.sync.dma_start(out=b1_sb[:], in_=b1.rearrange("(p j) -> p j", j=PACK))
         w2_rows = sbuf.tile([P, PACK, R], BF16)
-        nc.sync.dma_start(out=w2_rows[:], in_=w2.rearrange("(t p) r -> p t r", p=P))
+        nc.sync.dma_start(out=w2_rows[:], in_=w2.rearrange("(p t) r -> p t r", t=PACK))
         b2_sb = sbuf.tile([P, R], BF16)
         nc.sync.dma_start(out=b2_sb[:], in_=b2.partition_broadcast(P))
 
@@ -90,14 +85,8 @@ def tile_treemlpv3_pa_s_kernel(tc, x, w1, b1, w2, b2, out):
             .unsqueeze(4)
             .to_broadcast([P, WINDOW_ROWS, 2, WINDOW_COLS, 2]),
         )
-        ident_bf = sbuf.tile([P, P], BF16)
-        nc.vector.tensor_copy(out=ident_bf[:], in_=ident[:])
 
-        x_words = (
-            x_sb[:].rearrange("r c k -> r (c k)").bitcast(F32).rearrange(
-                "r (c p u) -> r c u p", c=LEVELS, u=2
-            )
-        )
+        x_words = x_sb[:].bitcast(F32).rearrange("r (c p u) -> r c u p", c=LEVELS, u=2)
         xT = [bank(c, [P, 2, P], F32, "xT_%d" % c) for c in range(LEVELS)]
 
         def transpose_x(c):
@@ -105,17 +94,16 @@ def tile_treemlpv3_pa_s_kernel(tc, x, w1, b1, w2, b2, out):
                 nc.tensor.transpose(xT[c][:, u, :], x_words[:, c, u, :], ident[:])
 
         warm_up = bank(3, [P, P], F32, "warm_up_0")
-        for n in range(3):
+        for n in range(2):
             nc.tensor.matmul(warm_up[:], lhsT=ident[:], rhs=ident[:], start=True, stop=True)
         transpose_x(0)
-        x_level0 = x_sb[:, 0, :].rearrange("r (p t) -> r t p", t=PACK)
+        x_level0 = x_sb[:, 0:R].rearrange("r (p t) -> r t p", t=PACK)
         meanT = bank(2, [P, PACK, P], BF16, "meanT")
         for t in range(PACK):
             nc.tensor.matmul(
                 meanT[:, t, :], lhsT=x_level0[:, t, :], rhs=mean_of[:], start=True, stop=True
             )
-        biasT = bank(3, [P, P], BF16, "biasT")
-        nc.tensor.transpose(biasT[:], bias_rows[:], ident_bf[:])
+        transpose_x(1)
 
         X0, X1, MEAN0 = 0, 1, 2
         m_grouped = sbuf.tile([P, 3, P * PACK], BF16, align_bytes=64)
@@ -135,6 +123,15 @@ def tile_treemlpv3_pa_s_kernel(tc, x, w1, b1, w2, b2, out):
             regroup(nc.vector.tensor_copy, grouped[:, vector_share, :], rows[:, :, vector_share])
             regroup(nc.scalar.copy, grouped[:, scalar_share, :], rows[:, :, scalar_share])
 
+        def regroup_w1_chunk(c, n):
+            grouped = w1_grouped[:, c, n * CHUNK : (n + 1) * CHUNK, :].rearrange(
+                "p (i m) t -> p m t i", i=2
+            )
+            rows = w1_rows[:, c].rearrange("p t (m i) -> p m t i", i=PACK)[:, :, :, 2 * n : 2 * n + 2]
+            cut = VECTOR_COLS // 2
+            nc.vector.tensor_copy(out=grouped[:, 0:cut], in_=rows[:, 0:cut])
+            nc.scalar.copy(out=grouped[:, cut:P], in_=rows[:, cut:P])
+
         def quantise_chunk(codes, scales, grouped, n):
             cols = slice(n * CHUNK, (n + 1) * CHUNK)
             nc.vector.quantize_mx(
@@ -149,15 +146,15 @@ def tile_treemlpv3_pa_s_kernel(tc, x, w1, b1, w2, b2, out):
                 in_=xT[c][:].rearrange("p u r -> p r u"),
             )
 
-        def quantise_merged(b):
+        def quantise_merged(first, last):
             nc.vector.quantize_mx(
-                out=m_codes[:, b, :].bitcast(FP8X4), scales=m_scales[:, b, :], in_=m_grouped[:, b, :]
+                out=m_codes[:, first : last + 1, :].rearrange("p b r -> p (b r)").bitcast(FP8X4),
+                scales=m_scales[:, first : last + 1, :].rearrange("p b r -> p (b r)"),
+                in_=m_grouped[:, first : last + 1, :].rearrange("p b k -> p (b k)"),
             )
 
         copy_xT(nc.vector.tensor_copy, 0)
-        quantise_merged(X0)
-        b1_sb = sbuf.tile([P, PACK], BF16)
-        nc.scalar.copy(out=b1_sb[:], in_=biasT[:, 0:PACK])
+        quantise_merged(X0, X0)
 
         hid_acc = {}
 
@@ -182,18 +179,17 @@ def tile_treemlpv3_pa_s_kernel(tc, x, w1, b1, w2, b2, out):
                     stop=(c == LEVELS - 1),
                 )
 
-        regroup_chunk(w1_grouped[:, 0], w1_rows[:, 0], 0, VECTOR_COLS)
-        regroup_chunk(w1_grouped[:, 0], w1_rows[:, 0], 1, VECTOR_COLS)
+        regroup_w1_chunk(0, 0)
+        regroup_w1_chunk(0, 1)
         nc.scalar.copy(
             out=m_grouped[:, MEAN0, :].rearrange("p (r t) -> p r t", t=PACK),
             in_=meanT[:].rearrange("p t r -> p r t"),
         )
         quantise_chunk(w1_codes[:, 0], w1_scales[:, 0], w1_grouped[:, 0], 0)
         quantise_chunk(w1_codes[:, 0], w1_scales[:, 0], w1_grouped[:, 0], 1)
-        quantise_merged(MEAN0)
 
-        def keep_warm(n, passes):
-            spare = bank(3, [P, P], F32, "spare_%d" % n)
+        def keep_warm(n, name, passes):
+            spare = bank(n, [P, P], F32, name)
             for k in range(passes):
                 nc.tensor.matmul_mx(
                     out=spare[:],
@@ -205,15 +201,14 @@ def tile_treemlpv3_pa_s_kernel(tc, x, w1, b1, w2, b2, out):
                     stop=True,
                 )
 
-        keep_warm(0, 6)
-        transpose_x(1)
+        keep_warm(3, "spare_0", 6)
         first_product(0, 0, range(0, 2))
         first_product(0, 0, range(2, 4))
-        keep_warm(1, 4)
+        keep_warm(3, "spare_1", 4)
         copy_xT(nc.scalar.copy, 1)
-        regroup_chunk(w1_grouped[:, 1], w1_rows[:, 1], 0, VECTOR_COLS)
-        regroup_chunk(w1_grouped[:, 1], w1_rows[:, 1], 1, VECTOR_COLS)
-        quantise_merged(X1)
+        regroup_w1_chunk(1, 0)
+        regroup_w1_chunk(1, 1)
+        quantise_merged(X1, MEAN0)
         open_level(1)
         first_product(0, 1, range(0, 4))
         quantise_chunk(w1_codes[:, 1], w1_scales[:, 1], w1_grouped[:, 1], 0)
@@ -254,6 +249,7 @@ def tile_treemlpv3_pa_s_kernel(tc, x, w1, b1, w2, b2, out):
         gelu(0)
         regroup_chunk(w2_grouped, w2_rows, 1, VECTOR_COLS)
         gelu(1)
+        keep_warm(4, "spare_2", 6)
         quantise_chunk(w2_codes, w2_scales, w2_grouped, 0)
         regroup(nc.vector.tensor_copy, hid_grouped[0][:], hid_rows[0][:])
         quantise_chunk(w2_codes, w2_scales, w2_grouped, 1)

@@ -23,7 +23,9 @@ WINDOW_COLS = 4
 BANKS = 8
 
 CHUNK = 256
-VECTOR_COLS = 160
+VECTOR_COLS_W1 = (160, 128)
+VECTOR_COLS_W2 = 160
+VECTOR_COLS_HID1 = 80
 
 FLOPS = 2 * LEVELS * P * (LEVELS * R * F + F * R)
 
@@ -97,13 +99,13 @@ def tile_treemlpv3_pa_s_kernel(tc, x, w1, b1, w2, b2, out):
         for n in range(2):
             nc.tensor.matmul(warm_up[:], lhsT=ident[:], rhs=ident[:], start=True, stop=True)
         transpose_x(0)
+        transpose_x(1)
         x_level0 = x_sb[:, 0:R].rearrange("r (p t) -> r t p", t=PACK)
         meanT = bank(2, [P, PACK, P], BF16, "meanT")
         for t in range(PACK):
             nc.tensor.matmul(
                 meanT[:, t, :], lhsT=x_level0[:, t, :], rhs=mean_of[:], start=True, stop=True
             )
-        transpose_x(1)
 
         X0, X1, MEAN0 = 0, 1, 2
         m_grouped = sbuf.tile([P, 3, P * PACK], BF16, align_bytes=64)
@@ -128,7 +130,7 @@ def tile_treemlpv3_pa_s_kernel(tc, x, w1, b1, w2, b2, out):
                 "p (i m) t -> p m t i", i=2
             )
             rows = w1_rows[:, c].rearrange("p t (m i) -> p m t i", i=PACK)[:, :, :, 2 * n : 2 * n + 2]
-            cut = VECTOR_COLS // 2
+            cut = VECTOR_COLS_W1[c] // 2
             nc.vector.tensor_copy(out=grouped[:, 0:cut], in_=rows[:, 0:cut])
             nc.scalar.copy(out=grouped[:, cut:P], in_=rows[:, cut:P])
 
@@ -154,6 +156,7 @@ def tile_treemlpv3_pa_s_kernel(tc, x, w1, b1, w2, b2, out):
             )
 
         copy_xT(nc.vector.tensor_copy, 0)
+        copy_xT(nc.scalar.copy, 1)
         quantise_merged(X0, X0)
 
         hid_acc = {}
@@ -205,7 +208,6 @@ def tile_treemlpv3_pa_s_kernel(tc, x, w1, b1, w2, b2, out):
         first_product(0, 0, range(0, 2))
         first_product(0, 0, range(2, 4))
         keep_warm(3, "spare_1", 4)
-        copy_xT(nc.scalar.copy, 1)
         regroup_w1_chunk(1, 0)
         regroup_w1_chunk(1, 1)
         quantise_merged(X1, MEAN0)
@@ -245,16 +247,18 @@ def tile_treemlpv3_pa_s_kernel(tc, x, w1, b1, w2, b2, out):
                 in_=hid_grouped[i][:].rearrange("p r t -> p (r t)"),
             )
 
-        regroup_chunk(w2_grouped, w2_rows, 0, VECTOR_COLS)
+        regroup_chunk(w2_grouped, w2_rows, 0, VECTOR_COLS_W2)
+        regroup_chunk(w2_grouped, w2_rows, 1, VECTOR_COLS_W2)
         gelu(0)
-        regroup_chunk(w2_grouped, w2_rows, 1, VECTOR_COLS)
         gelu(1)
         keep_warm(4, "spare_2", 6)
         quantise_chunk(w2_codes, w2_scales, w2_grouped, 0)
         regroup(nc.vector.tensor_copy, hid_grouped[0][:], hid_rows[0][:])
         quantise_chunk(w2_codes, w2_scales, w2_grouped, 1)
         quantise_hid(0)
-        regroup(nc.vector.tensor_copy, hid_grouped[1][:], hid_rows[1][:])
+        cut = VECTOR_COLS_HID1
+        regroup(nc.vector.tensor_copy, hid_grouped[1][:, 0:cut], hid_rows[1][:, :, 0:cut])
+        regroup(nc.scalar.copy, hid_grouped[1][:, cut:P], hid_rows[1][:, :, cut:P])
         quantise_hid(1)
 
         out_rows = out.rearrange("b h w l r -> (b h w) l r")

from contextlib import ExitStack

import concourse.masks as masks
import concourse.mybir as mybir

F32 = mybir.dt.float32
BF16 = mybir.dt.bfloat16
U32 = mybir.dt.uint32
U8 = mybir.dt.uint8
FP8X4 = mybir.dt.float8_e4m3fn_x4
ACT = mybir.ActivationFunctionType
ALU = mybir.AluOpType
AXIS = mybir.AxisListType

P = 128
PACK = 4
K_PASS = P * PACK
LEVELS = 2
R = 512
F = 512
WINDOW_ROWS = 8
WINDOW_COLS = 4
BANKS = 8

CHUNK = 256
VECTOR_COLS_W1 = (160, 128)
VECTOR_COLS_W2 = 160
VECTOR_COLS_HID1 = 80

FLOPS = 2 * LEVELS * P * (LEVELS * R * F + F * R)


def regroup(copy, grouped, rows):
    copy(
        out=grouped.rearrange("p (g i) t -> p g t i", i=4),
        in_=rows.rearrange("p t (g i) -> p g t i", i=4),
    )


def tile_treemlpv3_pa_s_kernel(tc, x, w1, b1, w2, b2, out):
    nc = tc.nc

    with ExitStack() as ctx:
        sbuf = ctx.enter_context(tc.tile_pool(name="sbuf", bufs=1))
        psum = ctx.enter_context(tc.psum_pool(name="psum", bufs=1))
        ctx.enter_context(tc.manual_schedule())

        def bank(n, shape, dtype, name):
            return psum.tile(shape, dtype, name=name, tag="bank%d" % n)

        table_in = sbuf.tile([P, 1], F32)
        nc.vector.memset(table_in[:], 0.0)
        table_out = sbuf.tile([P, 1], F32)
        nc.scalar.activation(out=table_out[:], in_=table_in[:], func=ACT.Gelu_apprx_tanh)

        x_sb = sbuf.tile([P, LEVELS * R], BF16)
        nc.sync.dma_start(out=x_sb[:], in_=x.rearrange("b h w l r -> (b h w) (l r)"))
        w1_rows = sbuf.tile([P, LEVELS, PACK, F], BF16)
        for c in range(LEVELS):
            nc.sync.dma_start(
                out=w1_rows[:, c],
                in_=w1[c * K_PASS : (c + 1) * K_PASS, :].rearrange("(p t) f -> p t f", t=PACK),
            )
        b1_sb = sbuf.tile([P, PACK], BF16)
        nc.sync.dma_start(out=b1_sb[:], in_=b1.rearrange("(p j) -> p j", j=PACK))
        w2_rows = sbuf.tile([P, PACK, R], BF16)
        nc.sync.dma_start(out=w2_rows[:], in_=w2.rearrange("(p t) r -> p t r", t=PACK))
        b2_sb = sbuf.tile([P, R], BF16)
        nc.sync.dma_start(out=b2_sb[:], in_=b2.partition_broadcast(P))

        ident = sbuf.tile([P, P], F32)
        masks.make_identity(nc, ident[:])
        in_window = sbuf.tile([P, WINDOW_ROWS, WINDOW_COLS], F32)
        nc.vector.tensor_reduce(
            out=in_window[:],
            in_=ident[:].rearrange("p (a h c w) -> p a c h w", a=WINDOW_ROWS, h=2, w=2),
            axis=AXIS.XY,
            op=ALU.add,
        )
        quarter = sbuf.tile([P, WINDOW_ROWS, WINDOW_COLS], F32)
        nc.vector.tensor_scalar_mul(out=quarter[:], in0=in_window[:], scalar1=0.25)
        mean_of = sbuf.tile([P, P], BF16)
        nc.vector.tensor_copy(
            out=mean_of[:].rearrange("p (a h c w) -> p a h c w", a=WINDOW_ROWS, h=2, w=2),
            in_=quarter[:]
            .unsqueeze(2)
            .unsqueeze(4)
            .to_broadcast([P, WINDOW_ROWS, 2, WINDOW_COLS, 2]),
        )

        x_words = x_sb[:].bitcast(F32).rearrange("r (c p u) -> r c u p", c=LEVELS, u=2)
        xT = [bank(c, [P, 2, P], F32, "xT_%d" % c) for c in range(LEVELS)]

        def transpose_x(c):
            for u in range(2):
                nc.tensor.transpose(xT[c][:, u, :], x_words[:, c, u, :], ident[:])

        warm_up = bank(3, [P, P], F32, "warm_up_0")
        for n in range(2):
            nc.tensor.matmul(warm_up[:], lhsT=ident[:], rhs=ident[:], start=True, stop=True)
        transpose_x(0)
        transpose_x(1)
        x_level0 = x_sb[:, 0:R].rearrange("r (p t) -> r t p", t=PACK)
        meanT = bank(2, [P, PACK, P], BF16, "meanT")
        for t in range(PACK):
            nc.tensor.matmul(
                meanT[:, t, :], lhsT=x_level0[:, t, :], rhs=mean_of[:], start=True, stop=True
            )

        X0, X1, MEAN0 = 0, 1, 2
        m_grouped = sbuf.tile([P, 3, P * PACK], BF16, align_bytes=64)
        m_codes = sbuf.tile([P, 3, P], U32, align_bytes=64)
        m_scales = sbuf.tile([P, 3, P], U8, align_bytes=64)
        w1_grouped = sbuf.tile([P, LEVELS, F, PACK], BF16, align_bytes=64)
        w1_codes = sbuf.tile([P, LEVELS, F], U32, align_bytes=64)
        w1_scales = sbuf.tile([P, LEVELS, F], U8, align_bytes=64)
        w2_grouped = sbuf.tile([P, R, PACK], BF16, align_bytes=64)
        w2_codes = sbuf.tile([P, R], U32, align_bytes=64)
        w2_scales = sbuf.tile([P, R], U8, align_bytes=64)

        def regroup_chunk(grouped, rows, n, vector_cols):
            cut = n * CHUNK + vector_cols
            vector_share = slice(n * CHUNK, cut)
            scalar_share = slice(cut, (n + 1) * CHUNK)
            regroup(nc.vector.tensor_copy, grouped[:, vector_share, :], rows[:, :, vector_share])
            regroup(nc.scalar.copy, grouped[:, scalar_share, :], rows[:, :, scalar_share])

        def regroup_w1_chunk(c, n):
            grouped = w1_grouped[:, c, n * CHUNK : (n + 1) * CHUNK, :].rearrange(
                "p (i m) t -> p m t i", i=2
            )
            rows = w1_rows[:, c].rearrange("p t (m i) -> p m t i", i=PACK)[:, :, :, 2 * n : 2 * n + 2]
            cut = VECTOR_COLS_W1[c] // 2
            nc.vector.tensor_copy(out=grouped[:, 0:cut], in_=rows[:, 0:cut])
            nc.scalar.copy(out=grouped[:, cut:P], in_=rows[:, cut:P])

        def quantise_chunk(codes, scales, grouped, n):
            cols = slice(n * CHUNK, (n + 1) * CHUNK)
            nc.vector.quantize_mx(
                out=codes[:, cols].bitcast(FP8X4),
                scales=scales[:, cols],
                in_=grouped[:, cols, :].rearrange("p f t -> p (f t)"),
            )

        def copy_xT(copy, c):
            copy(
                out=m_grouped[:, X0 + c, :].bitcast(F32).rearrange("p (r u) -> p r u", u=2),
                in_=xT[c][:].rearrange("p u r -> p r u"),
            )

        def quantise_merged(first, last):
            nc.vector.quantize_mx(
                out=m_codes[:, first : last + 1, :].rearrange("p b r -> p (b r)").bitcast(FP8X4),
                scales=m_scales[:, first : last + 1, :].rearrange("p b r -> p (b r)"),
                in_=m_grouped[:, first : last + 1, :].rearrange("p b k -> p (b k)"),
            )

        copy_xT(nc.vector.tensor_copy, 0)
        copy_xT(nc.scalar.copy, 1)
        quantise_merged(X0, X0)

        hid_acc = {}

        def open_level(i):
            for j in range(PACK):
                n = (BANKS // 2 + PACK * i + j) % BANKS
                hid_acc[i, j] = bank(n, [P, P], F32, "hid_acc_%d_%d" % (i, j))

        open_level(0)

        def first_product(c, i, js):
            block = X1 if c == 1 else (X0 if i == 0 else MEAN0)
            for j in js:
                chunk = slice(j * P, (j + 1) * P)
                nc.tensor.matmul_mx(
                    out=hid_acc[i, j][:],
                    lhsT=w1_codes[:, c, chunk].bitcast(FP8X4),
                    lhsT_scale=w1_scales[:, c, chunk],
                    rhs=m_codes[:, block, :].bitcast(FP8X4),
                    rhs_scale=m_scales[:, block, :],
                    start=(c == 0),
                    stop=(c == LEVELS - 1),
                )

        regroup_w1_chunk(0, 0)
        regroup_w1_chunk(0, 1)
        nc.scalar.copy(
            out=m_grouped[:, MEAN0, :].rearrange("p (r t) -> p r t", t=PACK),
            in_=meanT[:].rearrange("p t r -> p r t"),
        )
        quantise_chunk(w1_codes[:, 0], w1_scales[:, 0], w1_grouped[:, 0], 0)
        quantise_chunk(w1_codes[:, 0], w1_scales[:, 0], w1_grouped[:, 0], 1)

        def keep_warm(n, name, passes):
            spare = bank(n, [P, P], F32, name)
            for k in range(passes):
                nc.tensor.matmul_mx(
                    out=spare[:],
                    lhsT=m_codes[:, X0, :].bitcast(FP8X4),
                    lhsT_scale=m_scales[:, X0, :],
                    rhs=m_codes[:, X0, :].bitcast(FP8X4),
                    rhs_scale=m_scales[:, X0, :],
                    start=True,
                    stop=True,
                )

        keep_warm(3, "spare_0", 6)
        first_product(0, 0, range(0, 2))
        first_product(0, 0, range(2, 4))
        keep_warm(3, "spare_1", 4)
        regroup_w1_chunk(1, 0)
        regroup_w1_chunk(1, 1)
        quantise_merged(X1, MEAN0)
        open_level(1)
        first_product(0, 1, range(0, 4))
        quantise_chunk(w1_codes[:, 1], w1_scales[:, 1], w1_grouped[:, 1], 0)
        quantise_chunk(w1_codes[:, 1], w1_scales[:, 1], w1_grouped[:, 1], 1)
        first_product(1, 0, range(0, 2))
        first_product(1, 0, range(2, 4))
        first_product(1, 1, range(0, 4))

        hid_rows = [sbuf.tile([P, PACK, P], BF16, name="hid_rows_%d" % i) for i in range(LEVELS)]
        hid_grouped = [
            sbuf.tile([P, P, PACK], BF16, name="hid_grouped_%d" % i, align_bytes=64)
            for i in range(LEVELS)
        ]
        hid_codes = [
            sbuf.tile([P, P], U32, name="hid_codes_%d" % i, align_bytes=64) for i in range(LEVELS)
        ]
        hid_scales = [
            sbuf.tile([P, P], U8, name="hid_scales_%d" % i, align_bytes=64) for i in range(LEVELS)
        ]

        def gelu(i):
            for j in range(PACK):
                nc.scalar.activation(
                    out=hid_rows[i][:, j, :],
                    in_=hid_acc[i, j][:],
                    func=ACT.Gelu_apprx_tanh,
                    bias=b1_sb[:, j : j + 1],
                )

        def quantise_hid(i):
            nc.vector.quantize_mx(
                out=hid_codes[i][:].bitcast(FP8X4),
                scales=hid_scales[i][:],
                in_=hid_grouped[i][:].rearrange("p r t -> p (r t)"),
            )

        regroup_chunk(w2_grouped, w2_rows, 0, VECTOR_COLS_W2)
        regroup_chunk(w2_grouped, w2_rows, 1, VECTOR_COLS_W2)
        gelu(0)
        gelu(1)
        keep_warm(4, "spare_2", 6)
        quantise_chunk(w2_codes, w2_scales, w2_grouped, 0)
        regroup(nc.vector.tensor_copy, hid_grouped[0][:], hid_rows[0][:])
        quantise_chunk(w2_codes, w2_scales, w2_grouped, 1)
        quantise_hid(0)
        cut = VECTOR_COLS_HID1
        regroup(nc.vector.tensor_copy, hid_grouped[1][:, 0:cut], hid_rows[1][:, :, 0:cut])
        regroup(nc.scalar.copy, hid_grouped[1][:, cut:P], hid_rows[1][:, :, cut:P])
        quantise_hid(1)

        out_rows = out.rearrange("b h w l r -> (b h w) l r")
        for i in range(LEVELS):
            for n in range(R // CHUNK):
                cols = slice(n * CHUNK, (n + 1) * CHUNK)
                out_acc = bank(BANKS // 2 + 2 * i + n, [P, CHUNK], F32, "out_acc_%d_%d" % (i, n))
                nc.tensor.matmul_mx(
                    out=out_acc[:],
                    lhsT=hid_codes[i][:].bitcast(FP8X4),
                    lhsT_scale=hid_scales[i][:],
                    rhs=w2_codes[:, cols].bitcast(FP8X4),
                    rhs_scale=w2_scales[:, cols],
                    start=True,
                    stop=True,
                )
                result = sbuf.tile([P, CHUNK], F32, name="result_%d_%d" % (i, n))
                nc.vector.tensor_tensor(out=result[:], in0=out_acc[:], in1=b2_sb[:, cols], op=ALU.add)
                nc.sync.dma_start(out=out_rows[:, i, cols], in_=result[:])
